import numpy as np
import ml_dtypes


def mxq(x, axis, fmt="e4m3"):
    dtype, down = {"e4m3": (ml_dtypes.float8_e4m3fn, 7), "e5m2": (ml_dtypes.float8_e5m2, 14)}[fmt]
    v = np.moveaxis(np.asarray(x, np.float32).astype(ml_dtypes.bfloat16).astype(np.float64), axis, -1)
    blocks = v.reshape(v.shape[:-1] + (-1, 32))
    amax = np.abs(blocks).max(-1, keepdims=True)
    byte = np.maximum(np.where(amax > 0, np.frexp(amax)[1] - 1 + 127, 0) - down, 1)
    scale = np.exp2(byte - 127.0)
    codes = (blocks / scale).astype(np.float32).astype(dtype).astype(np.float64)
    return np.moveaxis((codes * scale).reshape(v.shape), -1, axis)


WIDE = False


def mx_kscale(k):
    if not WIDE:
        return np.ones(k)
    levels = np.array([10, -10, 5, -5, 0])
    if k % 512:
        return np.exp2(np.random.permutation(np.resize(levels, k // 32))).repeat(32)
    a = np.empty((k // 512, 16))
    for p in range(k // 512):
        a[p, :8] = np.random.permutation(np.resize(levels, 8))
        for g in range(8):
            far = levels[np.abs(levels - a[p, g]) >= 10]
            a[p, g + 8] = far[np.random.randint(len(far))]
    return np.exp2(a.ravel()).repeat(32)


BF16 = ml_dtypes.bfloat16


def bf(x):
    return np.asarray(x, np.float32).astype(BF16)


def f64(x):
    return np.asarray(x).astype(np.float64)


B, S, D, QC, KVC, FF = 1, 512, 1024, 8, 2, 4096
EPS = 1e-5


def rmsnorm(u, w):
    return u / np.sqrt(np.square(u).mean(-1, keepdims=True) + EPS) * w


def draw0():
    s = mx_kscale(D)
    t = np.exp2(np.round(np.log2(mx_kscale(FF)) / 2))
    return {"h_attn": bf(np.random.standard_normal((B, S, D)) * 1.3),
            "norm2_w": bf((1.0 + 0.1 * np.random.standard_normal(D)) * s),
            "ffn_wk": bf(np.random.standard_normal((D, FF)) / np.sqrt(D) / s[:, None] * t),
            "ffn_wv": bf(np.random.standard_normal((FF, D)) / np.sqrt(FF) / (t * t)[:, None])}


def core(h_attn, norm2_w, ffn_wk, ffn_wv):
    h = f64(h_attn)
    hn = rmsnorm(h, f64(norm2_w))
    k = np.square(np.maximum(mxq(hn, 2, "e4m3") @ mxq(f64(ffn_wk), 0, "e4m3"), 0.0))
    return h + (mxq(k, 2, "e4m3") @ mxq(f64(ffn_wv), 0, "e4m3"))


def e4m3fn_bytes(y):
    return np.clip(np.asarray(y, np.float64), -448.0, 448.0).astype(np.float32).astype(ml_dtypes.float8_e4m3fn).view(np.uint8)


def e4m3fn_values(b):
    return np.asarray(b, np.uint8).view(ml_dtypes.float8_e4m3fn).astype(np.float64)


def setup_inputs():
    d = draw0()
    x0 = np.asarray(d['ffn_wv']).astype(np.float64)
    s = (np.max(np.abs(x0), axis=(1,), keepdims=True) / 448.0).astype(np.float32)
    out = {}
    for k, v in d.items():
        if k == 'ffn_wv':
            out['ffn_wv_bytes'] = e4m3fn_bytes(x0 / s.astype(np.float64))
            out['ffn_wv_scale'] = s
        else:
            out[k] = v
    return out


def reference(h_attn, norm2_w, ffn_wk, ffn_wv_bytes, ffn_wv_scale):
    return core(h_attn, norm2_w, ffn_wk, e4m3fn_values(ffn_wv_bytes) * ffn_wv_scale.astype(np.float64))

@@ -1,0 +1,317 @@
+from contextlib import ExitStack
+
+import concourse.mybir as mybir
+from concourse.masks import make_identity
+
+S, D, FF = 512, 1024, 4096
+EPS = 1e-5
+FLOPS = 2 * 2 * S * D * FF
+
+F32 = mybir.dt.float32
+BF16 = mybir.dt.bfloat16
+U32 = mybir.dt.uint32
+U8 = mybir.dt.uint8
+FP8 = mybir.dt.float8_e4m3fn
+FP8X4 = mybir.dt.float8_e4m3fn_x4
+ALU = mybir.AluOpType
+ACT = mybir.ActivationFunctionType
+
+P = 128
+NT = S // P
+G = FF // 512
+Q = D // 512
+HALF = 512
+V_WIDENS = (8, 10)
+
+
+def tile_block_pc_kernel(tc, h_attn, norm2_w, ffn_wk, ffn_wv_bytes, ffn_wv_scale, out):
+    nc = tc.nc
+    h_v = h_attn.rearrange("b (i p) d -> (b i) p d", p=P)
+    out_v = out.rearrange("b (i p) d -> (b i) p d", p=P)
+    wk_v = ffn_wk.rearrange("(q p j) (g c) -> g q p j c", q=Q, p=P, j=4, c=512)
+    wv_v = ffn_wv_bytes.rearrange("(g p t) n -> g p t n", p=P, t=4)
+    sc_v = ffn_wv_scale.rearrange("(g p t) o -> p g (t o)", p=P, t=4)
+
+    with ExitStack() as ctx:
+        keep = ctx.enter_context(tc.tile_pool(name="keep", bufs=1))
+        wkraw = ctx.enter_context(tc.tile_pool(name="wkraw", bufs=4))
+        stage = ctx.enter_context(tc.tile_pool(name="stage", bufs=2))
+        wide3 = ctx.enter_context(tc.tile_pool(name="wide3", bufs=3))
+        psum = ctx.enter_context(tc.psum_pool(name="psum", bufs=4))
+        ctx.enter_context(tc.manual_schedule())
+
+        h_sb = keep.tile([P, NT, D], BF16, align_bytes=64, name="h_sb")
+        hcodes = keep.tile([P, NT, Q, P], U32, align_bytes=64, name="hcodes")
+        hscales = keep.tile([P, NT, Q, P], U8, align_bytes=64, name="hscales")
+        wvb = keep.tile([P, G, 4, D], U8, align_bytes=64, name="wvb")
+        sc = keep.tile([P, G, 4], F32, align_bytes=64, name="sc")
+        wvc = keep.tile([P, 2 * G, HALF], U32, align_bytes=64, name="wvc")
+        wvs = keep.tile([P, 2 * G, HALF], U8, align_bytes=64, name="wvs")
+        kc = keep.tile([P, G, S], U32, align_bytes=64, name="kc")
+        ks = keep.tile([P, G, S], U8, align_bytes=64, name="ks")
+        wrow = keep.tile([P, D], BF16, align_bytes=64, name="wrow")
+        ones = keep.tile([P, P], BF16, align_bytes=64, name="ones")
+        ident = keep.tile([P, P], F32, align_bytes=64, name="ident")
+        sumsq = keep.tile([P, NT], F32, align_bytes=64, name="sumsq")
+        rms = keep.tile([P, NT], F32, align_bytes=64, name="rms")
+        rstd = keep.tile([P, NT], F32, align_bytes=64, name="rstd")
+
+        nc.vector.memset(wrow[:], 0.0)
+        nc.vector.memset(ones[:], 1.0)
+        make_identity(nc, ident[:])
+
+        raw = {}
+
+        def load_wk(g):
+            raw[g] = wkraw.tile([P, Q, 4, 512], BF16, align_bytes=64, name="wkr")
+            for q in range(Q):
+                nc.sync.dma_start(out=raw[g][:, q, :, :], in_=wk_v[g, q])
+
+        def load_wv(g):
+            nc.sync.dma_start(out=wvb[:, g, :, :], in_=wv_v[g])
+
+        nc.sync.dma_start(out=h_sb[:, 0, :], in_=h_v[0])
+        nc.sync.dma_start(out=wrow[0:1, :], in_=norm2_w.rearrange("(o d) -> o d", o=1))
+        nc.sync.dma_start(out=h_sb[:, 1, :], in_=h_v[1])
+        load_wk(0)
+        nc.sync.dma_start(out=h_sb[:, 2, :], in_=h_v[2])
+        nc.sync.dma_start(out=h_sb[:, 3, :], in_=h_v[3])
+        nc.sync.dma_start(out=sc[:], in_=sc_v)
+        load_wv(0)
+        load_wk(1)
+        load_wv(1)
+        for g in range(2, 4):
+            load_wk(g)
+            load_wv(g)
+
+        grp, codes, scales = {}, {}, {}
+
+        def ia(g, q):
+            if q == 0:
+                grp[g] = stage.tile([P, Q, 2048], BF16, align_bytes=64, name="wkg")
+                codes[g] = wide3.tile([P, Q, 512], U32, align_bytes=64, name="wkc")
+                scales[g] = wide3.tile([P, Q, 512], U8, align_bytes=64, name="wks")
+            nc.vector.tensor_copy(
+                out=grp[g][:, q, :].rearrange("p (t m j) -> p m j t", t=4, j=4),
+                in_=raw[g][:, q, :, :].rearrange("p j (m t) -> p m j t", t=4),
+            )
+
+        def qa(g, q):
+            nc.vector.quantize_mx(out=codes[g][:, q, :].bitcast(FP8X4), scales=scales[g][:, q, :], in_=grp[g][:, q, :])
+
+        planes, wgrp = {}, {}
+
+        def widen(u, t):
+            g, half = u % G, u // G
+            if t == 0:
+                planes[u] = wide3.tile([P, 4, HALF], BF16, align_bytes=64, name="planes")
+            src = wvb[:, g, t, half * HALF:(half + 1) * HALF].bitcast(FP8)
+            if u in V_WIDENS:
+                nc.vector.tensor_scalar(out=planes[u][:, t, :], in0=src, scalar1=sc[:, g, t:t + 1], scalar2=None, op0=ALU.mult)
+            else:
+                nc.scalar.activation(out=planes[u][:, t, :], in_=src, func=ACT.Copy, scale=sc[:, g, t:t + 1])
+
+        def iv(u):
+            wgrp[u] = stage.tile([P, HALF * 4], BF16, align_bytes=64, name="wgrp")
+            nc.vector.tensor_copy(
+                out=wgrp[u][:].rearrange("p (c i t) -> p c t i", i=4, t=4),
+                in_=planes[u][:].rearrange("p t (c i) -> p c t i", i=4),
+            )
+
+        def qv(u):
+            nc.vector.quantize_mx(out=wvc[:, u, :].bitcast(FP8X4), scales=wvs[:, u, :], in_=wgrp[u][:])
+
+        r, kg = {}, {}
+        s1, acc = {}, {}
+
+        def t1(g, i):
+            s1[g, i] = psum.tile([P, 4, P], F32, name="s1")
+            for t in range(4):
+                for q in range(Q):
+                    nc.tensor.matmul_mx(
+                        out=s1[g, i][:, t, :],
+                        lhsT=codes[g][:, q, t * P:(t + 1) * P].bitcast(FP8X4),
+                        lhsT_scale=scales[g][:, q, t * P:(t + 1) * P],
+                        rhs=hcodes[:, i, q, :].bitcast(FP8X4),
+                        rhs_scale=hscales[:, i, q, :],
+                        start=(q == 0), stop=(q == Q - 1),
+                    )
+
+        def relu(g, i):
+            if i == 0:
+                r[g] = stage.tile([P, NT, P, 4], F32, align_bytes=64, name="r")
+            nc.scalar.activation(out=r[g][:, i, :, :], in_=s1[g, i][:].rearrange("p t n -> p n t"), func=ACT.Relu)
+
+        def sq(g, b):
+            if b == 0:
+                kg[g] = stage.tile([P, NT, P, 4], BF16, align_bytes=64, name="kg")
+            nc.scalar.activation(out=kg[g][:, 2 * b:2 * b + 2, :, :], in_=r[g][:, 2 * b:2 * b + 2, :, :], func=ACT.Square)
+
+        def qk(g):
+            nc.vector.quantize_mx(out=kc[:, g, :].bitcast(FP8X4), scales=ks[:, g, :], in_=kg[g][:].rearrange("p i n t -> p (i n t)"))
+
+        def t2(g, half, i):
+            if g == 0:
+                acc[half, i] = psum.tile([P, HALF], F32, name="acc" if half == 0 else "s1")
+            u = half * G + g
+            nc.tensor.matmul_mx(
+                out=acc[half, i][:],
+                lhsT=kc[:, g, i * P:(i + 1) * P].bitcast(FP8X4),
+                lhsT_scale=ks[:, g, i * P:(i + 1) * P],
+                rhs=wvc[:, u, :].bitcast(FP8X4),
+                rhs_scale=wvs[:, u, :],
+                start=(g == 0), stop=(g == G - 1),
+            )
+
+        def finish(half, i):
+            o = wide3.tile([P, HALF], F32, align_bytes=64, name="o")
+            cols = slice(half * HALF, (half + 1) * HALF)
+            nc.vector.tensor_tensor(out=o[:], in0=acc[half, i][:], in1=h_sb[:, i, cols], op=ALU.add)
+            nc.sync.dma_start(out=out_v[i][:, cols], in_=o[:])
+
+        wb = []
+        for c in range(2):
+            w_ps = psum.tile([P, 512], F32, name="acc")
+            nc.tensor.matmul(w_ps[:], lhsT=ones[:], rhs=wrow[:, c * 512:(c + 1) * 512], start=True, stop=True)
+            wb.append(w_ps)
+
+        def sumsquares(i):
+            junk = stage.tile([P, D], BF16, name="junk")
+            nc.scalar.activation(out=junk[:], in_=h_sb[:, i, :], func=ACT.Square, accum_out=sumsq[:, i:i + 1])
+
+        def rms_pair(a):
+            nc.vector.tensor_scalar(out=rms[:, a:a + 2], in0=sumsq[:, a:a + 2], scalar1=1.0 / D, scalar2=EPS, op0=ALU.mult, op1=ALU.add)
+            nc.scalar.activation(out=rms[:, a:a + 2], in_=rms[:, a:a + 2], func=ACT.Sqrt)
+            nc.vector.reciprocal(out=rstd[:, a:a + 2], in_=rms[:, a:a + 2])
+
+        hn = {}
+
+        def gain(i):
+            hn[i] = stage.tile([P, D], BF16, align_bytes=64, name="hn")
+            for c in range(2):
+                cols = slice(c * 512, (c + 1) * 512)
+                nc.vector.scalar_tensor_tensor(out=hn[i][:, cols], in0=h_sb[:, i, cols], scalar=rstd[:, i:i + 1], in1=wb[c][:], op0=ALU.mult, op1=ALU.mult)
+
+        tp, hg = {}, {}
+
+        def turn(i):
+            tp[i] = psum.tile([P, Q, 2, P], F32, name="s1")
+            words = hn[i][:].bitcast(F32)
+            for q in range(Q):
+                for v in range(2):
+                    nc.tensor.transpose(tp[i][:, q, v, :], words[:, 256 * q + v:256 * (q + 1):2], ident[:])
+
+        def turn_out(i):
+            hg[i] = stage.tile([P, Q * P * 4], BF16, align_bytes=64, name="hg")
+            nc.scalar.copy(out=hg[i][:].bitcast(F32).rearrange("p (q n v) -> p q n v", q=Q, v=2), in_=tp[i][:].rearrange("p q v n -> p q n v"))
+
+        def qh(i):
+            nc.vector.quantize_mx(
+                out=hcodes[:, i, :, :].rearrange("p q n -> p (q n)").bitcast(FP8X4),
+                scales=hscales[:, i, :, :].rearrange("p q n -> p (q n)"),
+                in_=hg[i][:],
+            )
+
+        sumsquares(0)
+        sumsquares(1)
+        ia(0, 0)
+        rms_pair(0)
+        sumsquares(2)
+        sumsquares(3)
+        gain(0)
+        gain(1)
+        turn(0)
+        turn(1)
+        ia(0, 1)
+        rms_pair(2)
+        qa(0, 0)
+        gain(2)
+        gain(3)
+        qa(0, 1)
+        turn_out(0)
+        turn_out(1)
+        turn(2)
+        turn(3)
+        ia(1, 0)
+        qh(0)
+        qh(1)
+        turn_out(2)
+        turn_out(3)
+        ia(1, 1)
+        qh(2)
+        qh(3)
+        for t in range(4):
+            widen(0, t)
+        qa(1, 0)
+        qa(1, 1)
+        iv(0)
+        for t in range(4):
+            widen(1, t)
+
+        todo_w = list(range(2, 2 * G))
+        todo_i = list(range(1, 2 * G))
+        todo_q = list(range(0, 2 * G))
+        for s in range(G):
+            n = 2 if s >= G - 2 else 1
+            if s + 4 < G:
+                load_wk(s + 4)
+                load_wv(s + 4)
+            ws = [todo_w.pop(0) for a in range(n)]
+            if s + 2 < G:
+                ia(s + 2, 0)
+            for i in range(NT):
+                t1(s, i)
+                relu(s, i)
+                if i == 0 and s > 0:
+                    sq(s - 1, 1)
+                if i == 2:
+                    sq(s, 0)
+                for u in ws:
+                    if u not in V_WIDENS:
+                        widen(u, i)
+                if s >= 2:
+                    t2(s - 2, 0, i)
+            qv(todo_q.pop(0))
+            if s + 2 < G:
+                ia(s + 2, 1)
+                qa(s + 2, 0)
+            iv(todo_i.pop(0))
+            if s + 2 < G:
+                qa(s + 2, 1)
+            for u in ws:
+                if u in V_WIDENS:
+                    for t in range(4):
+                        widen(u, t)
+            if s > 0:
+                qk(s - 1)
+            if n == 2:
+                qv(todo_q.pop(0))
+                iv(todo_i.pop(0))
+        sq(G - 1, 1)
+        for i in range(NT):
+            t2(G - 2, 0, i)
+        first = True
+        while todo_q:
+            if todo_w:
+                u = todo_w.pop(0)
+                for t in range(4):
+                    widen(u, t)
+            if todo_i:
+                iv(todo_i.pop(0))
+            u = todo_q.pop(0)
+            qv(u)
+            if first:
+                qk(G - 1)
+                for i in range(NT):
+                    t2(G - 1, 0, i)
+                for v in range(G, u):
+                    for i in range(NT):
+                        t2(v - G, 1, i)
+            for i in range(NT):
+                t2(u - G, 1, i)
+            if first:
+                for i in range(NT):
+                    finish(0, i)
+            first = False
+        for i in range(NT):
+            finish(1, i)

@@ -20,8 +20,11 @@ P = 128
 NT = S // P
 G = FF // 512
 Q = D // 512
-HALF = 512
-V_WIDENS = (8, 10)
+SLICES = ((0, 512), (512, 256), (768, 256))
+V_WIDENS = (2, 3, 4, 5, 6, 7, 9, 10, 11, 12, 14, 15, 16, 22, 23)
+PE_ITEMS = ((1, 0), (2, 0), (2, 1), (3, 0), (3, 1), (4, 0), (5, 0), (5, 1), (6, 0), (6, 1), (7, 1))
+S_ILS = (7, 19, 21, 23)
+EARLY = 3
 
 
 def tile_block_pc_kernel(tc, h_attn, norm2_w, ffn_wk, ffn_wv_bytes, ffn_wv_scale, out):
@@ -34,23 +37,24 @@ def tile_block_pc_kernel(tc, h_attn, norm2_w, ffn_wk, ffn_wv_bytes, ffn_wv_scale
 
     with ExitStack() as ctx:
         keep = ctx.enter_context(tc.tile_pool(name="keep", bufs=1))
-        wkraw = ctx.enter_context(tc.tile_pool(name="wkraw", bufs=4))
-        stage = ctx.enter_context(tc.tile_pool(name="stage", bufs=2))
-        wide3 = ctx.enter_context(tc.tile_pool(name="wide3", bufs=3))
-        psum = ctx.enter_context(tc.psum_pool(name="psum", bufs=4))
-        ctx.enter_context(tc.manual_schedule())
+        stage2 = ctx.enter_context(tc.tile_pool(name="stage2", bufs=2))
+        stage3 = ctx.enter_context(tc.tile_pool(name="stage3", bufs=3))
+        stage4 = ctx.enter_context(tc.tile_pool(name="stage4", bufs=4))
+        psum4 = ctx.enter_context(tc.psum_pool(name="psum4", bufs=4))
+        psum2 = ctx.enter_context(tc.psum_pool(name="psum2", bufs=2))
 
         h_sb = keep.tile([P, NT, D], BF16, align_bytes=64, name="h_sb")
         hcodes = keep.tile([P, NT, Q, P], U32, align_bytes=64, name="hcodes")
         hscales = keep.tile([P, NT, Q, P], U8, align_bytes=64, name="hscales")
         wvb = keep.tile([P, G, 4, D], U8, align_bytes=64, name="wvb")
         sc = keep.tile([P, G, 4], F32, align_bytes=64, name="sc")
-        wvc = keep.tile([P, 2 * G, HALF], U32, align_bytes=64, name="wvc")
-        wvs = keep.tile([P, 2 * G, HALF], U8, align_bytes=64, name="wvs")
+        wvc = keep.tile([P, G, D], U32, align_bytes=64, name="wvc")
+        wvs = keep.tile([P, G, D], U8, align_bytes=64, name="wvs")
         kc = keep.tile([P, G, S], U32, align_bytes=64, name="kc")
         ks = keep.tile([P, G, S], U8, align_bytes=64, name="ks")
         wrow = keep.tile([P, D], BF16, align_bytes=64, name="wrow")
         ones = keep.tile([P, P], BF16, align_bytes=64, name="ones")
+        identb = keep.tile([P, P], BF16, align_bytes=64, name="identb")
         ident = keep.tile([P, P], F32, align_bytes=64, name="ident")
         sumsq = keep.tile([P, NT], F32, align_bytes=64, name="sumsq")
         rms = keep.tile([P, NT], F32, align_bytes=64, name="rms")
@@ -59,73 +63,106 @@ def tile_block_pc_kernel(tc, h_attn, norm2_w, ffn_wk, ffn_wv_bytes, ffn_wv_scale
         nc.vector.memset(wrow[:], 0.0)
         nc.vector.memset(ones[:], 1.0)
         make_identity(nc, ident[:])
+        make_identity(nc, identb[:])
 
         raw = {}
 
-        def load_wk(g):
-            raw[g] = wkraw.tile([P, Q, 4, 512], BF16, align_bytes=64, name="wkr")
-            for q in range(Q):
-                nc.sync.dma_start(out=raw[g][:, q, :, :], in_=wk_v[g, q])
+        def load_wk(g, q, parts=1):
+            if q == 0:
+                raw[g] = stage3.tile([P, Q, 4, 512], BF16, align_bytes=64, name="wkr")
+            w = 512 // parts
+            for a in range(parts):
+                nc.sync.dma_start(out=raw[g][:, q, :, a * w:(a + 1) * w], in_=wk_v[g, q][:, :, a * w:(a + 1) * w])
 
         def load_wv(g):
             nc.sync.dma_start(out=wvb[:, g, :, :], in_=wv_v[g])
 
-        nc.sync.dma_start(out=h_sb[:, 0, :], in_=h_v[0])
+        def load_h(i):
+            nc.sync.dma_start(out=h_sb[:, i, :], in_=h_v[i])
+
+        load_h(0)
+        load_wk(0, 0, 2)
+        load_h(1)
         nc.sync.dma_start(out=wrow[0:1, :], in_=norm2_w.rearrange("(o d) -> o d", o=1))
-        nc.sync.dma_start(out=h_sb[:, 1, :], in_=h_v[1])
-        load_wk(0)
-        nc.sync.dma_start(out=h_sb[:, 2, :], in_=h_v[2])
-        nc.sync.dma_start(out=h_sb[:, 3, :], in_=h_v[3])
+        load_h(2)
+        load_h(3)
+        load_wk(0, 1)
         nc.sync.dma_start(out=sc[:], in_=sc_v)
         load_wv(0)
-        load_wk(1)
+        load_wk(1, 0)
+        load_wk(1, 1)
         load_wv(1)
-        for g in range(2, 4):
-            load_wk(g)
-            load_wv(g)
+        load_wk(2, 0)
+        load_wk(2, 1)
+        load_wv(2)
+        load_wv(3)
 
         grp, codes, scales = {}, {}, {}
 
-        def ia(g, q):
+        def pe_il(g, q):
+            for b in range(2):
+                bank = psum2.tile([P, 4, 64, 4], BF16, name="il")
+                for a in range(2):
+                    nc.tensor.matmul(
+                        bank[:, :, 32 * a:32 * a + 32, :].rearrange("p t m j -> p j m t"), lhsT=identb[:],
+                        rhs=raw[g][:, q, :, 256 * b + 128 * a:256 * b + 128 * a + 128].rearrange("p j (m t) -> p j m t", t=4),
+                        start=True, stop=True)
+                nc.scalar.copy(
+                    out=grp[g][:, q, :].bitcast(F32).rearrange("p (t w) -> p t w", t=4)[:, :, 128 * b:128 * b + 128],
+                    in_=bank[:].rearrange("p t m j -> p t (m j)").bitcast(F32))
+
+        def ia(g, q, parts=1):
             if q == 0:
-                grp[g] = stage.tile([P, Q, 2048], BF16, align_bytes=64, name="wkg")
-                codes[g] = wide3.tile([P, Q, 512], U32, align_bytes=64, name="wkc")
-                scales[g] = wide3.tile([P, Q, 512], U8, align_bytes=64, name="wks")
-            nc.vector.tensor_copy(
-                out=grp[g][:, q, :].rearrange("p (t m j) -> p m j t", t=4, j=4),
-                in_=raw[g][:, q, :, :].rearrange("p j (m t) -> p m j t", t=4),
-            )
+                grp[g] = stage2.tile([P, Q, 2048], BF16, align_bytes=64, name="wkg")
+                codes[g] = stage3.tile([P, Q, 512], U32, align_bytes=64, name="wkc")
+                scales[g] = stage3.tile([P, Q, 512], U8, align_bytes=64, name="wks")
+            if (g, q) in PE_ITEMS:
+                pe_il(g, q)
+                return
+            w = 128 // parts
+            for a in range(parts):
+                ms = slice(a * w, (a + 1) * w)
+                nc.vector.tensor_copy(
+                    out=grp[g][:, q, :].rearrange("p (t m j) -> p m j t", t=4, j=4)[:, ms, :, :],
+                    in_=raw[g][:, q, :, :].rearrange("p j (m t) -> p m j t", t=4)[:, ms, :, :],
+                )
 
         def qa(g, q):
             nc.vector.quantize_mx(out=codes[g][:, q, :].bitcast(FP8X4), scales=scales[g][:, q, :], in_=grp[g][:, q, :])
 
         planes, wgrp = {}, {}
 
-        def widen(u, t):
-            g, half = u % G, u // G
-            if t == 0:
-                planes[u] = wide3.tile([P, 4, HALF], BF16, align_bytes=64, name="planes")
-            src = wvb[:, g, t, half * HALF:(half + 1) * HALF].bitcast(FP8)
-            if u in V_WIDENS:
-                nc.vector.tensor_scalar(out=planes[u][:, t, :], in0=src, scalar1=sc[:, g, t:t + 1], scalar2=None, op0=ALU.mult)
-            else:
-                nc.scalar.activation(out=planes[u][:, t, :], in_=src, func=ACT.Copy, scale=sc[:, g, t:t + 1])
+        def widen(u):
+            c0, w = SLICES[u // G]
+            g = u % G
+            planes[u] = stage4.tile([P, 4, w], BF16, align_bytes=64, name="planes")
+            for t in range(4):
+                src = wvb[:, g, t, c0:c0 + w].bitcast(FP8)
+                if u in V_WIDENS:
+                    nc.vector.tensor_scalar(out=planes[u][:, t, :], in0=src, scalar1=sc[:, g, t:t + 1], scalar2=None, op0=ALU.mult)
+                else:
+                    nc.scalar.activation(out=planes[u][:, t, :], in_=src, func=ACT.Copy, scale=sc[:, g, t:t + 1])
 
         def iv(u):
-            wgrp[u] = stage.tile([P, HALF * 4], BF16, align_bytes=64, name="wgrp")
-            nc.vector.tensor_copy(
-                out=wgrp[u][:].rearrange("p (c i t) -> p c t i", i=4, t=4),
-                in_=planes[u][:].rearrange("p t (c i) -> p c t i", i=4),
-            )
+            c0, w = SLICES[u // G]
+            wgrp[u] = stage2.tile([P, w * 4], BF16, align_bytes=64, name="wgrp")
+            o_ap = wgrp[u][:].rearrange("p (c i t) -> p c t i", i=4, t=4)
+            i_ap = planes[u][:].rearrange("p t (c i) -> p c t i", i=4)
+            if u in S_ILS:
+                nc.scalar.copy(out=o_ap, in_=i_ap)
+            else:
+                nc.vector.tensor_copy(out=o_ap, in_=i_ap)
 
         def qv(u):
-            nc.vector.quantize_mx(out=wvc[:, u, :].bitcast(FP8X4), scales=wvs[:, u, :], in_=wgrp[u][:])
+            c0, w = SLICES[u // G]
+            g = u % G
+            nc.vector.quantize_mx(out=wvc[:, g, c0:c0 + w].bitcast(FP8X4), scales=wvs[:, g, c0:c0 + w], in_=wgrp[u][:])
 
         r, kg = {}, {}
         s1, acc = {}, {}
 
         def t1(g, i):
-            s1[g, i] = psum.tile([P, 4, P], F32, name="s1")
+            s1[g, i] = psum2.tile([P, 4, P], F32, name="s1")
             for t in range(4):
                 for q in range(Q):
                     nc.tensor.matmul_mx(
@@ -139,44 +176,48 @@ def tile_block_pc_kernel(tc, h_attn, norm2_w, ffn_wk, ffn_wv_bytes, ffn_wv_scale
 
         def relu(g, i):
             if i == 0:
-                r[g] = stage.tile([P, NT, P, 4], F32, align_bytes=64, name="r")
+                r[g] = stage2.tile([P, NT, P, 4], F32, align_bytes=64, name="r")
             nc.scalar.activation(out=r[g][:, i, :, :], in_=s1[g, i][:].rearrange("p t n -> p n t"), func=ACT.Relu)
 
         def sq(g, b):
             if b == 0:
-                kg[g] = stage.tile([P, NT, P, 4], BF16, align_bytes=64, name="kg")
+                kg[g] = stage2.tile([P, NT, P, 4], BF16, align_bytes=64, name="kg")
             nc.scalar.activation(out=kg[g][:, 2 * b:2 * b + 2, :, :], in_=r[g][:, 2 * b:2 * b + 2, :, :], func=ACT.Square)
 
         def qk(g):
             nc.vector.quantize_mx(out=kc[:, g, :].bitcast(FP8X4), scales=ks[:, g, :], in_=kg[g][:].rearrange("p i n t -> p (i n t)"))
 
-        def t2(g, half, i):
+        def t2(u, i):
+            c0, w = SLICES[u // G]
+            g, sl = u % G, u // G
             if g == 0:
-                acc[half, i] = psum.tile([P, HALF], F32, name="acc" if half == 0 else "s1")
-            u = half * G + g
+                if sl == 1:
+                    acc[sl, i] = psum2.tile([P, w], F32, name="il" if i < 2 else "s1")
+                else:
+                    acc[sl, i] = psum4.tile([P, w], F32, name="acc")
             nc.tensor.matmul_mx(
-                out=acc[half, i][:],
+                out=acc[sl, i][:],
                 lhsT=kc[:, g, i * P:(i + 1) * P].bitcast(FP8X4),
                 lhsT_scale=ks[:, g, i * P:(i + 1) * P],
-                rhs=wvc[:, u, :].bitcast(FP8X4),
-                rhs_scale=wvs[:, u, :],
+                rhs=wvc[:, g, c0:c0 + w].bitcast(FP8X4),
+                rhs_scale=wvs[:, g, c0:c0 + w],
                 start=(g == 0), stop=(g == G - 1),
             )
 
-        def finish(half, i):
-            o = wide3.tile([P, HALF], F32, align_bytes=64, name="o")
-            cols = slice(half * HALF, (half + 1) * HALF)
-            nc.vector.tensor_tensor(out=o[:], in0=acc[half, i][:], in1=h_sb[:, i, cols], op=ALU.add)
-            nc.sync.dma_start(out=out_v[i][:, cols], in_=o[:])
+        def finish(sl, i):
+            c0, w = SLICES[sl]
+            o = stage4.tile([P, w], F32, align_bytes=64, name="o")
+            nc.vector.tensor_tensor(out=o[:], in0=acc[sl, i][:], in1=h_sb[:, i, c0:c0 + w], op=ALU.add)
+            nc.sync.dma_start(out=out_v[i][:, c0:c0 + w], in_=o[:])
 
         wb = []
         for c in range(2):
-            w_ps = psum.tile([P, 512], F32, name="acc")
+            w_ps = psum4.tile([P, 512], F32, name="acc")
             nc.tensor.matmul(w_ps[:], lhsT=ones[:], rhs=wrow[:, c * 512:(c + 1) * 512], start=True, stop=True)
             wb.append(w_ps)
 
         def sumsquares(i):
-            junk = stage.tile([P, D], BF16, name="junk")
+            junk = stage2.tile([P, D], BF16, name="junk")
             nc.scalar.activation(out=junk[:], in_=h_sb[:, i, :], func=ACT.Square, accum_out=sumsq[:, i:i + 1])
 
         def rms_pair(a):
@@ -184,25 +225,23 @@ def tile_block_pc_kernel(tc, h_attn, norm2_w, ffn_wk, ffn_wv_bytes, ffn_wv_scale
             nc.scalar.activation(out=rms[:, a:a + 2], in_=rms[:, a:a + 2], func=ACT.Sqrt)
             nc.vector.reciprocal(out=rstd[:, a:a + 2], in_=rms[:, a:a + 2])
 
-        hn = {}
+        hn, tp, hg = {}, {}, {}
 
         def gain(i):
-            hn[i] = stage.tile([P, D], BF16, align_bytes=64, name="hn")
+            hn[i] = stage2.tile([P, D], BF16, align_bytes=64, name="hn")
             for c in range(2):
                 cols = slice(c * 512, (c + 1) * 512)
                 nc.vector.scalar_tensor_tensor(out=hn[i][:, cols], in0=h_sb[:, i, cols], scalar=rstd[:, i:i + 1], in1=wb[c][:], op0=ALU.mult, op1=ALU.mult)
 
-        tp, hg = {}, {}
-
         def turn(i):
-            tp[i] = psum.tile([P, Q, 2, P], F32, name="s1")
+            tp[i] = psum2.tile([P, Q, 2, P], F32, name="s1")
             words = hn[i][:].bitcast(F32)
             for q in range(Q):
                 for v in range(2):
                     nc.tensor.transpose(tp[i][:, q, v, :], words[:, 256 * q + v:256 * (q + 1):2], ident[:])
 
         def turn_out(i):
-            hg[i] = stage.tile([P, Q * P * 4], BF16, align_bytes=64, name="hg")
+            hg[i] = stage2.tile([P, Q * P * 4], BF16, align_bytes=64, name="hg")
             nc.scalar.copy(out=hg[i][:].bitcast(F32).rearrange("p (q n v) -> p q n v", q=Q, v=2), in_=tp[i][:].rearrange("p q v n -> p q n v"))
 
         def qh(i):
@@ -212,106 +251,76 @@ def tile_block_pc_kernel(tc, h_attn, norm2_w, ffn_wk, ffn_wv_bytes, ffn_wv_scale
                 in_=hg[i][:],
             )
 
-        sumsquares(0)
-        sumsquares(1)
-        ia(0, 0)
-        rms_pair(0)
-        sumsquares(2)
-        sumsquares(3)
-        gain(0)
-        gain(1)
-        turn(0)
-        turn(1)
-        ia(0, 1)
-        rms_pair(2)
-        qa(0, 0)
-        gain(2)
-        gain(3)
-        qa(0, 1)
-        turn_out(0)
-        turn_out(1)
-        turn(2)
-        turn(3)
+        for a in range(2):
+            sumsquares(2 * a)
+            sumsquares(2 * a + 1)
+            rms_pair(2 * a)
+            for i in (2 * a, 2 * a + 1):
+                gain(i)
+                turn(i)
+                turn_out(i)
+                qh(i)
+            ia(0, a, 2 - a)
+            qa(0, a)
         ia(1, 0)
-        qh(0)
-        qh(1)
-        turn_out(2)
-        turn_out(3)
-        ia(1, 1)
-        qh(2)
-        qh(3)
-        for t in range(4):
-            widen(0, t)
         qa(1, 0)
+        ia(1, 1)
         qa(1, 1)
-        iv(0)
-        for t in range(4):
-            widen(1, t)
+        for u in range(EARLY):
+            widen(u)
+        for u in range(EARLY - 1):
+            iv(u)
 
-        todo_w = list(range(2, 2 * G))
-        todo_i = list(range(1, 2 * G))
-        todo_q = list(range(0, 2 * G))
+        n_u = len(SLICES) * G
+        nw, ni, nq = EARLY, EARLY - 1, 0
+        sent = [0] * NT
+
+        def send(k_ready):
+            for i in range(NT):
+                while sent[i] < nq and sent[i] % G < k_ready:
+                    u = sent[i]
+                    if u >= G and u // G == 1 and k_ready < (6 if i < 2 else G):
+                        break
+                    t2(u, i)
+                    sent[i] += 1
+                    if u % G == G - 1:
+                        finish(u // G, i)
+
         for s in range(G):
-            n = 2 if s >= G - 2 else 1
-            if s + 4 < G:
-                load_wk(s + 4)
-                load_wv(s + 4)
-            ws = [todo_w.pop(0) for a in range(n)]
+            if s + 3 < G:
+                load_wk(s + 3, 0)
+                load_wk(s + 3, 1)
+            for g in (2 * s + 4, 2 * s + 5):
+                if g < G:
+                    load_wv(g)
             if s + 2 < G:
                 ia(s + 2, 0)
             for i in range(NT):
                 t1(s, i)
                 relu(s, i)
-                if i == 0 and s > 0:
-                    sq(s - 1, 1)
-                if i == 2:
-                    sq(s, 0)
-                for u in ws:
-                    if u not in V_WIDENS:
-                        widen(u, i)
-                if s >= 2:
-                    t2(s - 2, 0, i)
-            qv(todo_q.pop(0))
+                if i % 2 == 1:
+                    sq(s, i // 2)
             if s + 2 < G:
-                ia(s + 2, 1)
                 qa(s + 2, 0)
-            iv(todo_i.pop(0))
-            if s + 2 < G:
+                ia(s + 2, 1)
                 qa(s + 2, 1)
-            for u in ws:
-                if u in V_WIDENS:
-                    for t in range(4):
-                        widen(u, t)
-            if s > 0:
-                qk(s - 1)
-            if n == 2:
-                qv(todo_q.pop(0))
-                iv(todo_i.pop(0))
-        sq(G - 1, 1)
-        for i in range(NT):
-            t2(G - 2, 0, i)
-        first = True
-        while todo_q:
-            if todo_w:
-                u = todo_w.pop(0)
-                for t in range(4):
-                    widen(u, t)
-            if todo_i:
-                iv(todo_i.pop(0))
-            u = todo_q.pop(0)
-            qv(u)
-            if first:
-                qk(G - 1)
-                for i in range(NT):
-                    t2(G - 1, 0, i)
-                for v in range(G, u):
-                    for i in range(NT):
-                        t2(v - G, 1, i)
-            for i in range(NT):
-                t2(u - G, 1, i)
-            if first:
-                for i in range(NT):
-                    finish(0, i)
-            first = False
-        for i in range(NT):
-            finish(1, i)
+            qk(s)
+            for a in range(1 if s < 6 else 2):
+                qv(nq)
+                nq += 1
+                iv(ni)
+                ni += 1
+                widen(nw)
+                nw += 1
+            if s >= 1:
+                send(s)
+        while nq < n_u:
+            qv(nq)
+            nq += 1
+            if ni < n_u:
+                iv(ni)
+                ni += 1
+            if nw < n_u:
+                widen(nw)
+                nw += 1
+            send(G)

@@ -17,13 +17,16 @@ ALU = mybir.AluOpType
 ACT = mybir.ActivationFunctionType
 
 P = 128
+PACK = 4
+K_PASS = P * PACK
 NT = S // P
-G = FF // 512
-Q = D // 512
+G = FF // K_PASS
+Q = D // K_PASS
+
 SLICES = ((0, 512), (512, 256), (768, 256))
-V_WIDENS = (2, 3, 4, 5, 6, 7, 9, 10, 11, 12, 14, 15, 16, 22, 23)
-PE_ITEMS = ((1, 0), (2, 0), (2, 1), (3, 0), (3, 1), (4, 0), (5, 0), (5, 1), (6, 0), (6, 1), (7, 1))
-S_ILS = (7, 19, 21, 23)
+UNITS = [(g, 0, 512) for g in range(G)] + [(g, 512, 512) for g in range(G - 1)] + [(G - 1, 512, 256), (G - 1, 768, 256)]
+V_WIDENS = range(4, 11)
+PE_GROUPS = range(1, G)
 EARLY = 3
 
 
@@ -31,51 +34,54 @@ def tile_block_pc_kernel(tc, h_attn, norm2_w, ffn_wk, ffn_wv_bytes, ffn_wv_scale
     nc = tc.nc
     h_v = h_attn.rearrange("b (i p) d -> (b i) p d", p=P)
     out_v = out.rearrange("b (i p) d -> (b i) p d", p=P)
-    wk_v = ffn_wk.rearrange("(q p j) (g c) -> g q p j c", q=Q, p=P, j=4, c=512)
-    wv_v = ffn_wv_bytes.rearrange("(g p t) n -> g p t n", p=P, t=4)
-    sc_v = ffn_wv_scale.rearrange("(g p t) o -> p g (t o)", p=P, t=4)
+    wk_v = ffn_wk.rearrange("(q p j) (g c) -> g q p j c", q=Q, p=P, j=PACK, c=K_PASS)
+    wv_v = ffn_wv_bytes.rearrange("(g p t) n -> g p t n", p=P, t=PACK)
+    scale_v = ffn_wv_scale.rearrange("(g p t) o -> p g (t o)", p=P, t=PACK)
 
     with ExitStack() as ctx:
         keep = ctx.enter_context(tc.tile_pool(name="keep", bufs=1))
         stage2 = ctx.enter_context(tc.tile_pool(name="stage2", bufs=2))
         stage3 = ctx.enter_context(tc.tile_pool(name="stage3", bufs=3))
         stage4 = ctx.enter_context(tc.tile_pool(name="stage4", bufs=4))
+        stage8 = ctx.enter_context(tc.tile_pool(name="stage8", bufs=8))
         psum4 = ctx.enter_context(tc.psum_pool(name="psum4", bufs=4))
         psum2 = ctx.enter_context(tc.psum_pool(name="psum2", bufs=2))
 
         h_sb = keep.tile([P, NT, D], BF16, align_bytes=64, name="h_sb")
-        hcodes = keep.tile([P, NT, Q, P], U32, align_bytes=64, name="hcodes")
-        hscales = keep.tile([P, NT, Q, P], U8, align_bytes=64, name="hscales")
-        wvb = keep.tile([P, G, 4, D], U8, align_bytes=64, name="wvb")
-        sc = keep.tile([P, G, 4], F32, align_bytes=64, name="sc")
-        wvc = keep.tile([P, G, D], U32, align_bytes=64, name="wvc")
-        wvs = keep.tile([P, G, D], U8, align_bytes=64, name="wvs")
-        kc = keep.tile([P, G, S], U32, align_bytes=64, name="kc")
-        ks = keep.tile([P, G, S], U8, align_bytes=64, name="ks")
-        wrow = keep.tile([P, D], BF16, align_bytes=64, name="wrow")
+        h_codes = keep.tile([P, NT, Q, P], U32, align_bytes=64, name="h_codes")
+        h_scales = keep.tile([P, NT, Q, P], U8, align_bytes=64, name="h_scales")
+        wv_bytes = keep.tile([P, G, PACK, D], U8, align_bytes=64, name="wv_bytes")
+        wv_scale = keep.tile([P, G, PACK], F32, align_bytes=64, name="wv_scale")
+        wv_codes = keep.tile([P, G, D], U32, align_bytes=64, name="wv_codes")
+        wv_scales = keep.tile([P, G, D], U8, align_bytes=64, name="wv_scales")
+        k_codes = keep.tile([P, G, S], U32, align_bytes=64, name="k_codes")
+        k_scales = keep.tile([P, G, S], U8, align_bytes=64, name="k_scales")
+        gain_row = keep.tile([P, D], BF16, align_bytes=64, name="gain_row")
         ones = keep.tile([P, P], BF16, align_bytes=64, name="ones")
-        identb = keep.tile([P, P], BF16, align_bytes=64, name="identb")
-        ident = keep.tile([P, P], F32, align_bytes=64, name="ident")
+        ident_bf16 = keep.tile([P, P], BF16, align_bytes=64, name="ident_bf16")
+        ident_f32 = keep.tile([P, P], F32, align_bytes=64, name="ident_f32")
+        unused = keep.tile([P, D], BF16, align_bytes=64, name="unused")
         sumsq = keep.tile([P, NT], F32, align_bytes=64, name="sumsq")
         rms = keep.tile([P, NT], F32, align_bytes=64, name="rms")
         rstd = keep.tile([P, NT], F32, align_bytes=64, name="rstd")
 
-        nc.vector.memset(wrow[:], 0.0)
+        nc.vector.memset(gain_row[:], 0.0)
         nc.vector.memset(ones[:], 1.0)
-        make_identity(nc, ident[:])
-        make_identity(nc, identb[:])
+        make_identity(nc, ident_f32[:])
+        make_identity(nc, ident_bf16[:])
 
-        raw = {}
+        wk_raw = {}
 
         def load_wk(g, q, parts=1):
             if q == 0:
-                raw[g] = stage3.tile([P, Q, 4, 512], BF16, align_bytes=64, name="wkr")
-            w = 512 // parts
+                wk_raw[g] = stage3.tile([P, Q, PACK, K_PASS], BF16, align_bytes=64, name="wk_raw")
+            w = K_PASS // parts
             for a in range(parts):
-                nc.sync.dma_start(out=raw[g][:, q, :, a * w:(a + 1) * w], in_=wk_v[g, q][:, :, a * w:(a + 1) * w])
+                cols = slice(a * w, (a + 1) * w)
+                nc.sync.dma_start(out=wk_raw[g][:, q, :, cols], in_=wk_v[g, q][:, :, cols])
 
         def load_wv(g):
-            nc.sync.dma_start(out=wvb[:, g, :, :], in_=wv_v[g])
+            nc.sync.dma_start(out=wv_bytes[:, g, :, :], in_=wv_v[g])
 
         def load_h(i):
             nc.sync.dma_start(out=h_sb[:, i, :], in_=h_v[i])
@@ -83,244 +89,248 @@ def tile_block_pc_kernel(tc, h_attn, norm2_w, ffn_wk, ffn_wv_bytes, ffn_wv_scale
         load_h(0)
         load_wk(0, 0, 2)
         load_h(1)
-        nc.sync.dma_start(out=wrow[0:1, :], in_=norm2_w.rearrange("(o d) -> o d", o=1))
+        nc.sync.dma_start(out=gain_row[0:1, :], in_=norm2_w.rearrange("(o d) -> o d", o=1))
         load_h(2)
         load_h(3)
         load_wk(0, 1)
-        nc.sync.dma_start(out=sc[:], in_=sc_v)
+        nc.sync.dma_start(out=wv_scale[:], in_=scale_v)
         load_wv(0)
-        load_wk(1, 0)
-        load_wk(1, 1)
-        load_wv(1)
-        load_wk(2, 0)
-        load_wk(2, 1)
-        load_wv(2)
+        for g in (1, 2):
+            load_wk(g, 0)
+            load_wk(g, 1)
+            load_wv(g)
         load_wv(3)
+        load_wv(4)
 
-        grp, codes, scales = {}, {}, {}
+        wk_grouped, wk_codes, wk_scales = {}, {}, {}
 
-        def pe_il(g, q):
+        def new_wk(g):
+            if g not in wk_grouped:
+                wk_grouped[g] = stage2.tile([P, Q, K_PASS * PACK], BF16, align_bytes=64, name="wk_grouped")
+                wk_codes[g] = stage3.tile([P, Q, K_PASS], U32, align_bytes=64, name="wk_codes")
+                wk_scales[g] = stage3.tile([P, Q, K_PASS], U8, align_bytes=64, name="wk_scales")
+
+        def interleave_wk_on_tensor(g, q):
+            new_wk(g)
             for b in range(2):
-                bank = psum2.tile([P, 4, 64, 4], BF16, name="il")
+                bank = psum2.tile([P, PACK, 64, PACK], BF16, name="interleave")
                 for a in range(2):
+                    c0 = 256 * b + 128 * a
                     nc.tensor.matmul(
-                        bank[:, :, 32 * a:32 * a + 32, :].rearrange("p t m j -> p j m t"), lhsT=identb[:],
-                        rhs=raw[g][:, q, :, 256 * b + 128 * a:256 * b + 128 * a + 128].rearrange("p j (m t) -> p j m t", t=4),
-                        start=True, stop=True)
+                        bank[:, :, 32 * a:32 * a + 32, :].rearrange("p t m j -> p j m t"),
+                        lhsT=ident_bf16[:],
+                        rhs=wk_raw[g][:, q, :, c0:c0 + 128].rearrange("p j (m t) -> p j m t", t=PACK),
+                        start=True,
+                        stop=True,
+                    )
                 nc.scalar.copy(
-                    out=grp[g][:, q, :].bitcast(F32).rearrange("p (t w) -> p t w", t=4)[:, :, 128 * b:128 * b + 128],
-                    in_=bank[:].rearrange("p t m j -> p t (m j)").bitcast(F32))
+                    out=wk_grouped[g][:, q, :].bitcast(F32).rearrange("p (t w) -> p t w", t=PACK)[:, :, 128 * b:128 * b + 128],
+                    in_=bank[:].rearrange("p t m j -> p t (m j)").bitcast(F32),
+                )
 
-        def ia(g, q, parts=1):
-            if q == 0:
-                grp[g] = stage2.tile([P, Q, 2048], BF16, align_bytes=64, name="wkg")
-                codes[g] = stage3.tile([P, Q, 512], U32, align_bytes=64, name="wkc")
-                scales[g] = stage3.tile([P, Q, 512], U8, align_bytes=64, name="wks")
-            if (g, q) in PE_ITEMS:
-                pe_il(g, q)
-                return
-            w = 128 // parts
+        def interleave_wk_on_vector(g, q, parts=1):
+            new_wk(g)
+            w = P // parts
             for a in range(parts):
                 ms = slice(a * w, (a + 1) * w)
                 nc.vector.tensor_copy(
-                    out=grp[g][:, q, :].rearrange("p (t m j) -> p m j t", t=4, j=4)[:, ms, :, :],
-                    in_=raw[g][:, q, :, :].rearrange("p j (m t) -> p m j t", t=4)[:, ms, :, :],
+                    out=wk_grouped[g][:, q, :].rearrange("p (t m j) -> p m j t", t=PACK, j=PACK)[:, ms, :, :],
+                    in_=wk_raw[g][:, q, :, :].rearrange("p j (m t) -> p m j t", t=PACK)[:, ms, :, :],
                 )
 
-        def qa(g, q):
-            nc.vector.quantize_mx(out=codes[g][:, q, :].bitcast(FP8X4), scales=scales[g][:, q, :], in_=grp[g][:, q, :])
-
-        planes, wgrp = {}, {}
-
-        def widen(u):
-            c0, w = SLICES[u // G]
-            g = u % G
-            planes[u] = stage4.tile([P, 4, w], BF16, align_bytes=64, name="planes")
-            for t in range(4):
-                src = wvb[:, g, t, c0:c0 + w].bitcast(FP8)
-                if u in V_WIDENS:
-                    nc.vector.tensor_scalar(out=planes[u][:, t, :], in0=src, scalar1=sc[:, g, t:t + 1], scalar2=None, op0=ALU.mult)
+        def interleave_wk(g):
+            for q in range(Q):
+                if q == 0 and g in PE_GROUPS:
+                    interleave_wk_on_tensor(g, q)
                 else:
-                    nc.scalar.activation(out=planes[u][:, t, :], in_=src, func=ACT.Copy, scale=sc[:, g, t:t + 1])
+                    interleave_wk_on_vector(g, q)
 
-        def iv(u):
-            c0, w = SLICES[u // G]
-            wgrp[u] = stage2.tile([P, w * 4], BF16, align_bytes=64, name="wgrp")
-            o_ap = wgrp[u][:].rearrange("p (c i t) -> p c t i", i=4, t=4)
-            i_ap = planes[u][:].rearrange("p t (c i) -> p c t i", i=4)
-            if u in S_ILS:
-                nc.scalar.copy(out=o_ap, in_=i_ap)
-            else:
-                nc.vector.tensor_copy(out=o_ap, in_=i_ap)
+        def quantize_wk(g, q):
+            nc.vector.quantize_mx(
+                out=wk_codes[g][:, q, :].bitcast(FP8X4), scales=wk_scales[g][:, q, :], in_=wk_grouped[g][:, q, :])
 
-        def qv(u):
-            c0, w = SLICES[u // G]
-            g = u % G
-            nc.vector.quantize_mx(out=wvc[:, g, c0:c0 + w].bitcast(FP8X4), scales=wvs[:, g, c0:c0 + w], in_=wgrp[u][:])
+        wv_planes, wv_grouped = {}, {}
 
-        r, kg = {}, {}
-        s1, acc = {}, {}
+        def widen_wv(u):
+            g, c0, w = UNITS[u]
+            wv_planes[u] = stage4.tile([P, PACK, w], BF16, align_bytes=64, name="wv_planes")
+            for t in range(PACK):
+                values = wv_bytes[:, g, t, c0:c0 + w].bitcast(FP8)
+                scale = wv_scale[:, g, t:t + 1]
+                if u in V_WIDENS:
+                    nc.vector.tensor_scalar(
+                        out=wv_planes[u][:, t, :], in0=values, scalar1=scale, scalar2=None, op0=ALU.mult)
+                else:
+                    nc.scalar.activation(out=wv_planes[u][:, t, :], in_=values, func=ACT.Copy, scale=scale)
 
-        def t1(g, i):
-            s1[g, i] = psum2.tile([P, 4, P], F32, name="s1")
-            for t in range(4):
+        def interleave_wv(u):
+            w = UNITS[u][2]
+            wv_grouped[u] = stage2.tile([P, w * PACK], BF16, align_bytes=64, name="wv_grouped")
+            nc.vector.tensor_copy(
+                out=wv_grouped[u][:].rearrange("p (c i t) -> p c t i", i=4, t=PACK),
+                in_=wv_planes[u][:].rearrange("p t (c i) -> p c t i", i=4),
+            )
+
+        ready = [0] * len(SLICES)
+
+        def quantize_wv(u):
+            g, c0, w = UNITS[u]
+            nc.vector.quantize_mx(
+                out=wv_codes[:, g, c0:c0 + w].bitcast(FP8X4), scales=wv_scales[:, g, c0:c0 + w], in_=wv_grouped[u][:])
+            for sl in range(len(SLICES)):
+                if c0 <= SLICES[sl][0] < c0 + w:
+                    ready[sl] += 1
+
+        next_unit = {widen_wv: 0, interleave_wv: 0, quantize_wv: 0}
+
+        def advance(*jobs):
+            for job in jobs:
+                if next_unit[job] < len(UNITS):
+                    job(next_unit[job])
+                    next_unit[job] += 1
+
+        relu, k_grouped = {}, {}
+
+        def first_product(g, i):
+            bank = psum2.tile([P, PACK, P], F32, name="hidden")
+            for t in range(PACK):
                 for q in range(Q):
                     nc.tensor.matmul_mx(
-                        out=s1[g, i][:, t, :],
-                        lhsT=codes[g][:, q, t * P:(t + 1) * P].bitcast(FP8X4),
-                        lhsT_scale=scales[g][:, q, t * P:(t + 1) * P],
-                        rhs=hcodes[:, i, q, :].bitcast(FP8X4),
-                        rhs_scale=hscales[:, i, q, :],
-                        start=(q == 0), stop=(q == Q - 1),
+                        out=bank[:, t, :],
+                        lhsT=wk_codes[g][:, q, t * P:(t + 1) * P].bitcast(FP8X4),
+                        lhsT_scale=wk_scales[g][:, q, t * P:(t + 1) * P],
+                        rhs=h_codes[:, i, q, :].bitcast(FP8X4),
+                        rhs_scale=h_scales[:, i, q, :],
+                        start=(q == 0),
+                        stop=(q == Q - 1),
                     )
-
-        def relu(g, i):
             if i == 0:
-                r[g] = stage2.tile([P, NT, P, 4], F32, align_bytes=64, name="r")
-            nc.scalar.activation(out=r[g][:, i, :, :], in_=s1[g, i][:].rearrange("p t n -> p n t"), func=ACT.Relu)
+                relu[g] = stage2.tile([P, NT, P, PACK], F32, align_bytes=64, name="relu")
+                k_grouped[g] = stage2.tile([P, NT, P, PACK], BF16, align_bytes=64, name="k_grouped")
+            nc.scalar.activation(out=relu[g][:, i, :, :], in_=bank[:].rearrange("p t n -> p n t"), func=ACT.Relu)
 
-        def sq(g, b):
-            if b == 0:
-                kg[g] = stage2.tile([P, NT, P, 4], BF16, align_bytes=64, name="kg")
-            nc.scalar.activation(out=kg[g][:, 2 * b:2 * b + 2, :, :], in_=r[g][:, 2 * b:2 * b + 2, :, :], func=ACT.Square)
+        def square(g, first, last):
+            nc.scalar.activation(
+                out=k_grouped[g][:, first:last, :, :], in_=relu[g][:, first:last, :, :], func=ACT.Square)
 
-        def qk(g):
-            nc.vector.quantize_mx(out=kc[:, g, :].bitcast(FP8X4), scales=ks[:, g, :], in_=kg[g][:].rearrange("p i n t -> p (i n t)"))
+        def quantize_k(g):
+            nc.vector.quantize_mx(
+                out=k_codes[:, g, :].bitcast(FP8X4),
+                scales=k_scales[:, g, :],
+                in_=k_grouped[g][:].rearrange("p i n t -> p (i n t)"),
+            )
 
-        def t2(u, i):
-            c0, w = SLICES[u // G]
-            g, sl = u % G, u // G
+        acc = {}
+
+        def second_product(sl, g, i):
+            c0, w = SLICES[sl]
             if g == 0:
                 if sl == 1:
-                    acc[sl, i] = psum2.tile([P, w], F32, name="il" if i < 2 else "s1")
+                    acc[sl, i] = psum2.tile([P, w], F32, name="interleave" if i < 2 else "hidden")
                 else:
                     acc[sl, i] = psum4.tile([P, w], F32, name="acc")
             nc.tensor.matmul_mx(
                 out=acc[sl, i][:],
-                lhsT=kc[:, g, i * P:(i + 1) * P].bitcast(FP8X4),
-                lhsT_scale=ks[:, g, i * P:(i + 1) * P],
-                rhs=wvc[:, g, c0:c0 + w].bitcast(FP8X4),
-                rhs_scale=wvs[:, g, c0:c0 + w],
-                start=(g == 0), stop=(g == G - 1),
+                lhsT=k_codes[:, g, i * P:(i + 1) * P].bitcast(FP8X4),
+                lhsT_scale=k_scales[:, g, i * P:(i + 1) * P],
+                rhs=wv_codes[:, g, c0:c0 + w].bitcast(FP8X4),
+                rhs_scale=wv_scales[:, g, c0:c0 + w],
+                start=(g == 0),
+                stop=(g == G - 1),
             )
+            if g == G - 1:
+                result = (stage4 if sl == 0 else stage8).tile([P, w], F32, align_bytes=64, name="result")
+                nc.vector.tensor_tensor(out=result[:], in0=acc[sl, i][:], in1=h_sb[:, i, c0:c0 + w], op=ALU.add)
+                nc.sync.dma_start(out=out_v[i][:, c0:c0 + w], in_=result[:])
 
-        def finish(sl, i):
-            c0, w = SLICES[sl]
-            o = stage4.tile([P, w], F32, align_bytes=64, name="o")
-            nc.vector.tensor_tensor(out=o[:], in0=acc[sl, i][:], in1=h_sb[:, i, c0:c0 + w], op=ALU.add)
-            nc.sync.dma_start(out=out_v[i][:, c0:c0 + w], in_=o[:])
+        done = {(sl, i): 0 for sl in range(len(SLICES)) for i in range(NT)}
 
-        wb = []
+        def second_products(k_ready):
+            for sl in range(len(SLICES)):
+                for i in range(NT):
+                    if sl == 1 and k_ready < (G - 2 if i < 2 else G):
+                        continue
+                    if sl == 2 and done[0, i] < G:
+                        continue
+                    while done[sl, i] < min(ready[sl], k_ready):
+                        second_product(sl, done[sl, i], i)
+                        done[sl, i] += 1
+
+        gain_all = []
         for c in range(2):
-            w_ps = psum4.tile([P, 512], F32, name="acc")
-            nc.tensor.matmul(w_ps[:], lhsT=ones[:], rhs=wrow[:, c * 512:(c + 1) * 512], start=True, stop=True)
-            wb.append(w_ps)
+            bank = psum4.tile([P, 512], F32, name="acc")
+            nc.tensor.matmul(bank[:], lhsT=ones[:], rhs=gain_row[:, c * 512:(c + 1) * 512], start=True, stop=True)
+            gain_all.append(bank)
 
-        def sumsquares(i):
-            junk = stage2.tile([P, D], BF16, name="junk")
-            nc.scalar.activation(out=junk[:], in_=h_sb[:, i, :], func=ACT.Square, accum_out=sumsq[:, i:i + 1])
+        def sum_squares(i):
+            nc.scalar.activation(out=unused[:], in_=h_sb[:, i, :], func=ACT.Square, accum_out=sumsq[:, i:i + 1])
 
-        def rms_pair(a):
-            nc.vector.tensor_scalar(out=rms[:, a:a + 2], in0=sumsq[:, a:a + 2], scalar1=1.0 / D, scalar2=EPS, op0=ALU.mult, op1=ALU.add)
-            nc.scalar.activation(out=rms[:, a:a + 2], in_=rms[:, a:a + 2], func=ACT.Sqrt)
-            nc.vector.reciprocal(out=rstd[:, a:a + 2], in_=rms[:, a:a + 2])
+        def root(i0):
+            two = slice(i0, i0 + 2)
+            nc.vector.tensor_scalar(
+                out=rms[:, two], in0=sumsq[:, two], scalar1=1.0 / D, scalar2=EPS, op0=ALU.mult, op1=ALU.add)
+            nc.scalar.activation(out=rms[:, two], in_=rms[:, two], func=ACT.Sqrt)
+            nc.vector.reciprocal(out=rstd[:, two], in_=rms[:, two])
 
-        hn, tp, hg = {}, {}, {}
-
-        def gain(i):
-            hn[i] = stage2.tile([P, D], BF16, align_bytes=64, name="hn")
+        def normalize(i):
+            hn = stage2.tile([P, D], BF16, align_bytes=64, name="hn")
             for c in range(2):
                 cols = slice(c * 512, (c + 1) * 512)
-                nc.vector.scalar_tensor_tensor(out=hn[i][:, cols], in0=h_sb[:, i, cols], scalar=rstd[:, i:i + 1], in1=wb[c][:], op0=ALU.mult, op1=ALU.mult)
-
-        def turn(i):
-            tp[i] = psum2.tile([P, Q, 2, P], F32, name="s1")
-            words = hn[i][:].bitcast(F32)
+                nc.vector.scalar_tensor_tensor(
+                    out=hn[:, cols], in0=h_sb[:, i, cols], scalar=rstd[:, i:i + 1], in1=gain_all[c][:],
+                    op0=ALU.mult, op1=ALU.mult)
+            turned = psum2.tile([P, Q, 2, P], F32, name="hidden")
+            words = hn[:].bitcast(F32)
             for q in range(Q):
                 for v in range(2):
-                    nc.tensor.transpose(tp[i][:, q, v, :], words[:, 256 * q + v:256 * (q + 1):2], ident[:])
-
-        def turn_out(i):
-            hg[i] = stage2.tile([P, Q * P * 4], BF16, align_bytes=64, name="hg")
-            nc.scalar.copy(out=hg[i][:].bitcast(F32).rearrange("p (q n v) -> p q n v", q=Q, v=2), in_=tp[i][:].rearrange("p q v n -> p q n v"))
-
-        def qh(i):
+                    nc.tensor.transpose(turned[:, q, v, :], words[:, 256 * q + v:256 * (q + 1):2], ident_f32[:])
+            hn_grouped = stage2.tile([P, Q * P * PACK], BF16, align_bytes=64, name="hn_grouped")
+            nc.scalar.copy(
+                out=hn_grouped[:].bitcast(F32).rearrange("p (q n v) -> p q n v", q=Q, v=2),
+                in_=turned[:].rearrange("p q v n -> p q n v"),
+            )
             nc.vector.quantize_mx(
-                out=hcodes[:, i, :, :].rearrange("p q n -> p (q n)").bitcast(FP8X4),
-                scales=hscales[:, i, :, :].rearrange("p q n -> p (q n)"),
-                in_=hg[i][:],
+                out=h_codes[:, i, :, :].rearrange("p q n -> p (q n)").bitcast(FP8X4),
+                scales=h_scales[:, i, :, :].rearrange("p q n -> p (q n)"),
+                in_=hn_grouped[:],
             )
 
         for a in range(2):
-            sumsquares(2 * a)
-            sumsquares(2 * a + 1)
-            rms_pair(2 * a)
-            for i in (2 * a, 2 * a + 1):
-                gain(i)
-                turn(i)
-                turn_out(i)
-                qh(i)
-            ia(0, a, 2 - a)
-            qa(0, a)
-        ia(1, 0)
-        qa(1, 0)
-        ia(1, 1)
-        qa(1, 1)
+            sum_squares(2 * a)
+            sum_squares(2 * a + 1)
+            root(2 * a)
+            normalize(2 * a)
+            normalize(2 * a + 1)
+            interleave_wk_on_vector(0, a, 2 - a)
+            quantize_wk(0, a)
+        interleave_wk(1)
+        for q in range(Q):
+            quantize_wk(1, q)
         for u in range(EARLY):
-            widen(u)
+            advance(widen_wv)
         for u in range(EARLY - 1):
-            iv(u)
+            advance(interleave_wv)
 
-        n_u = len(SLICES) * G
-        nw, ni, nq = EARLY, EARLY - 1, 0
-        sent = [0] * NT
-
-        def send(k_ready):
+        for g in range(G):
+            if g + 3 < G:
+                load_wk(g + 3, 0)
+                load_wk(g + 3, 1)
+            for later in (2 * g + 5, 2 * g + 6):
+                if later < G:
+                    load_wv(later)
             for i in range(NT):
-                while sent[i] < nq and sent[i] % G < k_ready:
-                    u = sent[i]
-                    if u >= G and u // G == 1 and k_ready < (6 if i < 2 else G):
-                        break
-                    t2(u, i)
-                    sent[i] += 1
-                    if u % G == G - 1:
-                        finish(u // G, i)
-
-        for s in range(G):
-            if s + 3 < G:
-                load_wk(s + 3, 0)
-                load_wk(s + 3, 1)
-            for g in (2 * s + 4, 2 * s + 5):
-                if g < G:
-                    load_wv(g)
-            if s + 2 < G:
-                ia(s + 2, 0)
-            for i in range(NT):
-                t1(s, i)
-                relu(s, i)
+                first_product(g, i)
                 if i % 2 == 1:
-                    sq(s, i // 2)
-            if s + 2 < G:
-                qa(s + 2, 0)
-                ia(s + 2, 1)
-                qa(s + 2, 1)
-            qk(s)
-            for a in range(1 if s < 6 else 2):
-                qv(nq)
-                nq += 1
-                iv(ni)
-                ni += 1
-                widen(nw)
-                nw += 1
-            if s >= 1:
-                send(s)
-        while nq < n_u:
-            qv(nq)
-            nq += 1
-            if ni < n_u:
-                iv(ni)
-                ni += 1
-            if nw < n_u:
-                widen(nw)
-                nw += 1
-            send(G)
+                    square(g, i - 1, i + 1)
+            if g + 2 < G:
+                interleave_wk(g + 2)
+            quantize_k(g)
+            second_products(g + 1)
+            advance(quantize_wv, interleave_wv, widen_wv)
+            if g + 2 < G:
+                for q in range(Q):
+                    quantize_wk(g + 2, q)
+
+        while next_unit[quantize_wv] < len(UNITS):
+            advance(quantize_wv, interleave_wv, widen_wv)
+            second_products(G)

from contextlib import ExitStack

import concourse.mybir as mybir
from concourse.masks import make_identity

S, D, FF = 512, 1024, 4096
EPS = 1e-5
FLOPS = 2 * 2 * S * D * FF

F32 = mybir.dt.float32
BF16 = mybir.dt.bfloat16
U32 = mybir.dt.uint32
U8 = mybir.dt.uint8
FP8 = mybir.dt.float8_e4m3fn
FP8X4 = mybir.dt.float8_e4m3fn_x4
ALU = mybir.AluOpType
ACT = mybir.ActivationFunctionType

P = 128
PACK = 4
K_PASS = P * PACK
NT = S // P
G = FF // K_PASS
Q = D // K_PASS

SLICES = ((0, 512), (512, 256), (768, 256))
UNITS = [(g, 0, 512) for g in range(G)] + [(g, 512, 512) for g in range(G - 1)] + [(G - 1, 512, 256), (G - 1, 768, 256)]
V_WIDENS = range(4, 11)
PE_GROUPS = range(1, G)
EARLY = 3


def tile_block_pc_kernel(tc, h_attn, norm2_w, ffn_wk, ffn_wv_bytes, ffn_wv_scale, out):
    nc = tc.nc
    h_v = h_attn.rearrange("b (i p) d -> (b i) p d", p=P)
    out_v = out.rearrange("b (i p) d -> (b i) p d", p=P)
    wk_v = ffn_wk.rearrange("(q p j) (g c) -> g q p j c", q=Q, p=P, j=PACK, c=K_PASS)
    wv_v = ffn_wv_bytes.rearrange("(g p t) n -> g p t n", p=P, t=PACK)
    scale_v = ffn_wv_scale.rearrange("(g p t) o -> p g (t o)", p=P, t=PACK)

    with ExitStack() as ctx:
        keep = ctx.enter_context(tc.tile_pool(name="keep", bufs=1))
        stage2 = ctx.enter_context(tc.tile_pool(name="stage2", bufs=2))
        stage3 = ctx.enter_context(tc.tile_pool(name="stage3", bufs=3))
        stage4 = ctx.enter_context(tc.tile_pool(name="stage4", bufs=4))
        stage8 = ctx.enter_context(tc.tile_pool(name="stage8", bufs=8))
        psum4 = ctx.enter_context(tc.psum_pool(name="psum4", bufs=4))
        psum2 = ctx.enter_context(tc.psum_pool(name="psum2", bufs=2))

        h_sb = keep.tile([P, NT, D], BF16, align_bytes=64, name="h_sb")
        h_codes = keep.tile([P, NT, Q, P], U32, align_bytes=64, name="h_codes")
        h_scales = keep.tile([P, NT, Q, P], U8, align_bytes=64, name="h_scales")
        wv_bytes = keep.tile([P, G, PACK, D], U8, align_bytes=64, name="wv_bytes")
        wv_scale = keep.tile([P, G, PACK], F32, align_bytes=64, name="wv_scale")
        wv_codes = keep.tile([P, G, D], U32, align_bytes=64, name="wv_codes")
        wv_scales = keep.tile([P, G, D], U8, align_bytes=64, name="wv_scales")
        k_codes = keep.tile([P, G, S], U32, align_bytes=64, name="k_codes")
        k_scales = keep.tile([P, G, S], U8, align_bytes=64, name="k_scales")
        gain_row = keep.tile([P, D], BF16, align_bytes=64, name="gain_row")
        ones = keep.tile([P, P], BF16, align_bytes=64, name="ones")
        ident_bf16 = keep.tile([P, P], BF16, align_bytes=64, name="ident_bf16")
        ident_f32 = keep.tile([P, P], F32, align_bytes=64, name="ident_f32")
        unused = keep.tile([P, D], BF16, align_bytes=64, name="unused")
        sumsq = keep.tile([P, NT], F32, align_bytes=64, name="sumsq")
        rms = keep.tile([P, NT], F32, align_bytes=64, name="rms")
        rstd = keep.tile([P, NT], F32, align_bytes=64, name="rstd")

        nc.vector.memset(gain_row[:], 0.0)
        nc.vector.memset(ones[:], 1.0)
        make_identity(nc, ident_f32[:])
        make_identity(nc, ident_bf16[:])

        wk_raw = {}

        def load_wk(g, q, parts=1):
            if q == 0:
                wk_raw[g] = stage3.tile([P, Q, PACK, K_PASS], BF16, align_bytes=64, name="wk_raw")
            w = K_PASS // parts
            for a in range(parts):
                cols = slice(a * w, (a + 1) * w)
                nc.sync.dma_start(out=wk_raw[g][:, q, :, cols], in_=wk_v[g, q][:, :, cols])

        def load_wv(g):
            nc.sync.dma_start(out=wv_bytes[:, g, :, :], in_=wv_v[g])

        def load_h(i):
            nc.sync.dma_start(out=h_sb[:, i, :], in_=h_v[i])

        load_h(0)
        load_wk(0, 0, 2)
        load_h(1)
        nc.sync.dma_start(out=gain_row[0:1, :], in_=norm2_w.rearrange("(o d) -> o d", o=1))
        load_h(2)
        load_h(3)
        load_wk(0, 1)
        nc.sync.dma_start(out=wv_scale[:], in_=scale_v)
        load_wv(0)
        for g in (1, 2):
            load_wk(g, 0)
            load_wk(g, 1)
            load_wv(g)
        load_wv(3)
        load_wv(4)

        wk_grouped, wk_codes, wk_scales = {}, {}, {}

        def new_wk(g):
            if g not in wk_grouped:
                wk_grouped[g] = stage2.tile([P, Q, K_PASS * PACK], BF16, align_bytes=64, name="wk_grouped")
                wk_codes[g] = stage3.tile([P, Q, K_PASS], U32, align_bytes=64, name="wk_codes")
                wk_scales[g] = stage3.tile([P, Q, K_PASS], U8, align_bytes=64, name="wk_scales")

        def interleave_wk_on_tensor(g, q):
            new_wk(g)
            for b in range(2):
                bank = psum2.tile([P, PACK, 64, PACK], BF16, name="interleave")
                for a in range(2):
                    c0 = 256 * b + 128 * a
                    nc.tensor.matmul(
                        bank[:, :, 32 * a:32 * a + 32, :].rearrange("p t m j -> p j m t"),
                        lhsT=ident_bf16[:],
                        rhs=wk_raw[g][:, q, :, c0:c0 + 128].rearrange("p j (m t) -> p j m t", t=PACK),
                        start=True,
                        stop=True,
                    )
                nc.scalar.copy(
                    out=wk_grouped[g][:, q, :].bitcast(F32).rearrange("p (t w) -> p t w", t=PACK)[:, :, 128 * b:128 * b + 128],
                    in_=bank[:].rearrange("p t m j -> p t (m j)").bitcast(F32),
                )

        def interleave_wk_on_vector(g, q, parts=1):
            new_wk(g)
            w = P // parts
            for a in range(parts):
                ms = slice(a * w, (a + 1) * w)
                nc.vector.tensor_copy(
                    out=wk_grouped[g][:, q, :].rearrange("p (t m j) -> p m j t", t=PACK, j=PACK)[:, ms, :, :],
                    in_=wk_raw[g][:, q, :, :].rearrange("p j (m t) -> p m j t", t=PACK)[:, ms, :, :],
                )

        def interleave_wk(g):
            for q in range(Q):
                if q == 0 and g in PE_GROUPS:
                    interleave_wk_on_tensor(g, q)
                else:
                    interleave_wk_on_vector(g, q)

        def quantize_wk(g, q):
            nc.vector.quantize_mx(
                out=wk_codes[g][:, q, :].bitcast(FP8X4), scales=wk_scales[g][:, q, :], in_=wk_grouped[g][:, q, :])

        wv_planes, wv_grouped = {}, {}

        def widen_wv(u):
            g, c0, w = UNITS[u]
            wv_planes[u] = stage4.tile([P, PACK, w], BF16, align_bytes=64, name="wv_planes")
            for t in range(PACK):
                values = wv_bytes[:, g, t, c0:c0 + w].bitcast(FP8)
                scale = wv_scale[:, g, t:t + 1]
                if u in V_WIDENS:
                    nc.vector.tensor_scalar(
                        out=wv_planes[u][:, t, :], in0=values, scalar1=scale, scalar2=None, op0=ALU.mult)
                else:
                    nc.scalar.activation(out=wv_planes[u][:, t, :], in_=values, func=ACT.Copy, scale=scale)

        def interleave_wv(u):
            w = UNITS[u][2]
            wv_grouped[u] = stage2.tile([P, w * PACK], BF16, align_bytes=64, name="wv_grouped")
            nc.vector.tensor_copy(
                out=wv_grouped[u][:].rearrange("p (c i t) -> p c t i", i=4, t=PACK),
                in_=wv_planes[u][:].rearrange("p t (c i) -> p c t i", i=4),
            )

        ready = [0] * len(SLICES)

        def quantize_wv(u):
            g, c0, w = UNITS[u]
            nc.vector.quantize_mx(
                out=wv_codes[:, g, c0:c0 + w].bitcast(FP8X4), scales=wv_scales[:, g, c0:c0 + w], in_=wv_grouped[u][:])
            for sl in range(len(SLICES)):
                if c0 <= SLICES[sl][0] < c0 + w:
                    ready[sl] += 1

        next_unit = {widen_wv: 0, interleave_wv: 0, quantize_wv: 0}

        def advance(*jobs):
            for job in jobs:
                if next_unit[job] < len(UNITS):
                    job(next_unit[job])
                    next_unit[job] += 1

        relu, k_grouped = {}, {}

        def first_product(g, i):
            bank = psum2.tile([P, PACK, P], F32, name="hidden")
            for t in range(PACK):
                for q in range(Q):
                    nc.tensor.matmul_mx(
                        out=bank[:, t, :],
                        lhsT=wk_codes[g][:, q, t * P:(t + 1) * P].bitcast(FP8X4),
                        lhsT_scale=wk_scales[g][:, q, t * P:(t + 1) * P],
                        rhs=h_codes[:, i, q, :].bitcast(FP8X4),
                        rhs_scale=h_scales[:, i, q, :],
                        start=(q == 0),
                        stop=(q == Q - 1),
                    )
            if i == 0:
                relu[g] = stage2.tile([P, NT, P, PACK], F32, align_bytes=64, name="relu")
                k_grouped[g] = stage2.tile([P, NT, P, PACK], BF16, align_bytes=64, name="k_grouped")
            nc.scalar.activation(out=relu[g][:, i, :, :], in_=bank[:].rearrange("p t n -> p n t"), func=ACT.Relu)

        def square(g, first, last):
            nc.scalar.activation(
                out=k_grouped[g][:, first:last, :, :], in_=relu[g][:, first:last, :, :], func=ACT.Square)

        def quantize_k(g):
            nc.vector.quantize_mx(
                out=k_codes[:, g, :].bitcast(FP8X4),
                scales=k_scales[:, g, :],
                in_=k_grouped[g][:].rearrange("p i n t -> p (i n t)"),
            )

        acc = {}

        def second_product(sl, g, i):
            c0, w = SLICES[sl]
            if g == 0:
                if sl == 1:
                    acc[sl, i] = psum2.tile([P, w], F32, name="interleave" if i < 2 else "hidden")
                else:
                    acc[sl, i] = psum4.tile([P, w], F32, name="acc")
            nc.tensor.matmul_mx(
                out=acc[sl, i][:],
                lhsT=k_codes[:, g, i * P:(i + 1) * P].bitcast(FP8X4),
                lhsT_scale=k_scales[:, g, i * P:(i + 1) * P],
                rhs=wv_codes[:, g, c0:c0 + w].bitcast(FP8X4),
                rhs_scale=wv_scales[:, g, c0:c0 + w],
                start=(g == 0),
                stop=(g == G - 1),
            )
            if g == G - 1:
                result = (stage4 if sl == 0 else stage8).tile([P, w], F32, align_bytes=64, name="result")
                nc.vector.tensor_tensor(out=result[:], in0=acc[sl, i][:], in1=h_sb[:, i, c0:c0 + w], op=ALU.add)
                nc.sync.dma_start(out=out_v[i][:, c0:c0 + w], in_=result[:])

        done = {(sl, i): 0 for sl in range(len(SLICES)) for i in range(NT)}

        def second_products(k_ready):
            for sl in range(len(SLICES)):
                for i in range(NT):
                    if sl == 1 and k_ready < (G - 2 if i < 2 else G):
                        continue
                    if sl == 2 and done[0, i] < G:
                        continue
                    while done[sl, i] < min(ready[sl], k_ready):
                        second_product(sl, done[sl, i], i)
                        done[sl, i] += 1

        gain_all = []
        for c in range(2):
            bank = psum4.tile([P, 512], F32, name="acc")
            nc.tensor.matmul(bank[:], lhsT=ones[:], rhs=gain_row[:, c * 512:(c + 1) * 512], start=True, stop=True)
            gain_all.append(bank)

        def sum_squares(i):
            nc.scalar.activation(out=unused[:], in_=h_sb[:, i, :], func=ACT.Square, accum_out=sumsq[:, i:i + 1])

        def root(i0):
            two = slice(i0, i0 + 2)
            nc.vector.tensor_scalar(
                out=rms[:, two], in0=sumsq[:, two], scalar1=1.0 / D, scalar2=EPS, op0=ALU.mult, op1=ALU.add)
            nc.scalar.activation(out=rms[:, two], in_=rms[:, two], func=ACT.Sqrt)
            nc.vector.reciprocal(out=rstd[:, two], in_=rms[:, two])

        def normalize(i):
            hn = stage2.tile([P, D], BF16, align_bytes=64, name="hn")
            for c in range(2):
                cols = slice(c * 512, (c + 1) * 512)
                nc.vector.scalar_tensor_tensor(
                    out=hn[:, cols], in0=h_sb[:, i, cols], scalar=rstd[:, i:i + 1], in1=gain_all[c][:],
                    op0=ALU.mult, op1=ALU.mult)
            turned = psum2.tile([P, Q, 2, P], F32, name="hidden")
            words = hn[:].bitcast(F32)
            for q in range(Q):
                for v in range(2):
                    nc.tensor.transpose(turned[:, q, v, :], words[:, 256 * q + v:256 * (q + 1):2], ident_f32[:])
            hn_grouped = stage2.tile([P, Q * P * PACK], BF16, align_bytes=64, name="hn_grouped")
            nc.scalar.copy(
                out=hn_grouped[:].bitcast(F32).rearrange("p (q n v) -> p q n v", q=Q, v=2),
                in_=turned[:].rearrange("p q v n -> p q n v"),
            )
            nc.vector.quantize_mx(
                out=h_codes[:, i, :, :].rearrange("p q n -> p (q n)").bitcast(FP8X4),
                scales=h_scales[:, i, :, :].rearrange("p q n -> p (q n)"),
                in_=hn_grouped[:],
            )

        for a in range(2):
            sum_squares(2 * a)
            sum_squares(2 * a + 1)
            root(2 * a)
            normalize(2 * a)
            normalize(2 * a + 1)
            interleave_wk_on_vector(0, a, 2 - a)
            quantize_wk(0, a)
        interleave_wk(1)
        for q in range(Q):
            quantize_wk(1, q)
        for u in range(EARLY):
            advance(widen_wv)
        for u in range(EARLY - 1):
            advance(interleave_wv)

        for g in range(G):
            if g + 3 < G:
                load_wk(g + 3, 0)
                load_wk(g + 3, 1)
            for later in (2 * g + 5, 2 * g + 6):
                if later < G:
                    load_wv(later)
            for i in range(NT):
                first_product(g, i)
                if i % 2 == 1:
                    square(g, i - 1, i + 1)
            if g + 2 < G:
                interleave_wk(g + 2)
            quantize_k(g)
            second_products(g + 1)
            advance(quantize_wv, interleave_wv, widen_wv)
            if g + 2 < G:
                for q in range(Q):
                    quantize_wk(g + 2, q)

        while next_unit[quantize_wv] < len(UNITS):
            advance(quantize_wv, interleave_wv, widen_wv)
            second_products(G)
